import numpy as np
import ml_dtypes


def mxq(x, axis, fmt="e4m3"):
    dtype, down = {"e4m3": (ml_dtypes.float8_e4m3fn, 7), "e5m2": (ml_dtypes.float8_e5m2, 14)}[fmt]
    v = np.moveaxis(np.asarray(x, np.float32).astype(ml_dtypes.bfloat16).astype(np.float64), axis, -1)
    blocks = v.reshape(v.shape[:-1] + (-1, 32))
    amax = np.abs(blocks).max(-1, keepdims=True)
    byte = np.maximum(np.where(amax > 0, np.frexp(amax)[1] - 1 + 127, 0) - down, 1)
    scale = np.exp2(byte - 127.0)
    codes = (blocks / scale).astype(np.float32).astype(dtype).astype(np.float64)
    return np.moveaxis((codes * scale).reshape(v.shape), -1, axis)


WIDE = False


def mx_kscale(k):
    if not WIDE:
        return np.ones(k)
    levels = np.array([10, -10, 5, -5, 0])
    if k % 512:
        return np.exp2(np.random.permutation(np.resize(levels, k // 32))).repeat(32)
    a = np.empty((k // 512, 16))
    for p in range(k // 512):
        a[p, :8] = np.random.permutation(np.resize(levels, 8))
        for g in range(8):
            far = levels[np.abs(levels - a[p, g]) >= 10]
            a[p, g + 8] = far[np.random.randint(len(far))]
    return np.exp2(a.ravel()).repeat(32)


BF16 = ml_dtypes.bfloat16


def bf(x):
    return np.asarray(x, np.float32).astype(BF16)


def f64(x):
    return np.asarray(x).astype(np.float64)


N, CH = 10240, 512

REPARAM_OFFSET = 2.0 ** (-18)
PEDESTAL = REPARAM_OFFSET ** 2
BETA_MIN = 1e-6
BETA_BOUND = (BETA_MIN + PEDESTAL) ** 0.5
GAMMA_BOUND = REPARAM_OFFSET


def setup_inputs():
    u = np.exp2(np.round(np.log2(mx_kscale(CH)) / 2))
    amp = np.exp(0.6 * np.random.standard_normal((N, 1)))
    x = np.random.standard_normal((N, CH)) * amp * u
    beta = (0.7 + 0.7 * np.random.standard_normal(CH)) * u
    gamma = np.random.standard_normal((CH, CH)) * np.sqrt(2.0 / CH) * u[:, None] / u[None, :]
    return {"x": bf(x), "beta": bf(beta), "gamma": bf(gamma)}


def reference(x, beta, gamma):
    x = f64(x)
    b = np.maximum(f64(beta), BETA_BOUND) ** 2 - PEDESTAL
    g = np.maximum(f64(gamma), GAMMA_BOUND) ** 2 - PEDESTAL
    norm = np.sqrt((mxq(x * x, 1, "e4m3") @ mxq(g, 1, "e4m3").T) + b)
    return x / norm

@@ -1,0 +1,246 @@
+from contextlib import ExitStack
+
+import concourse.masks as masks
+import concourse.mybir as mybir
+
+F32 = mybir.dt.float32
+BF16 = mybir.dt.bfloat16
+U32 = mybir.dt.uint32
+U8 = mybir.dt.uint8
+FP8X4 = mybir.dt.float8_e4m3fn_x4
+ACT = mybir.ActivationFunctionType
+ALU = mybir.AluOpType
+
+P = 128
+N_ROWS = 10240
+CH = 512
+CHUNK = 512
+NCH = N_ROWS // CHUNK
+FLOPS = 2 * N_ROWS * CH * CH
+
+PEDESTAL = 2.0 ** -36
+BETA_BOUND = (1e-6 + PEDESTAL) ** 0.5
+
+PL = 3
+QL = 2
+NM = 3
+NR = 3
+NSQ = 6
+NCD = 4
+NRT = 3
+NO = 4
+NTMP = 3
+
+
+HEAD = 4
+
+
+def head_engine(c, h):
+    if h == 1 and c != 1:
+        return "V"
+    return "S"
+
+
+def tile_gdn_t_kernel(tc, x, beta, gamma, out):
+    nc = tc.nc
+    with ExitStack() as ctx:
+        keep = ctx.enter_context(tc.tile_pool(name="keep", bufs=1))
+        psum = ctx.enter_context(tc.psum_pool(name="psum", bufs=1))
+        ctx.enter_context(tc.manual_schedule())
+
+        ident = keep.tile([P, P], F32, name="ident")
+        warm = keep.tile([P, 1], F32, name="warm")
+        warm2 = keep.tile([P, 1], F32, name="warm2")
+        gam = keep.tile([P, 4, CH], BF16, name="gam")
+        bet = keep.tile([4, P], BF16, name="bet")
+        bz = keep.tile([P, P], F32, name="bz")
+        b1 = keep.tile([P, 4], F32, name="b1")
+        b2 = keep.tile([P, 4], F32, name="b2")
+        b_sb = keep.tile([P, 4], F32, name="b_sb")
+        gw = [keep.tile([P, 1024], BF16, name="gw%d" % i) for i in range(2)]
+        g2 = [keep.tile([P, 1024], F32, name="g2%d" % i) for i in range(2)]
+        gq = keep.tile([P, 2048], BF16, name="gq", align_bytes=64)
+        g_cd = keep.tile([P, CH], U32, name="g_cd", align_bytes=64)
+        g_sc = keep.tile([P, CH], U8, name="g_sc", align_bytes=64)
+        xs = [keep.tile([P, 4, CH], BF16, name="x%d" % c) for c in range(NCH)]
+        sq = [keep.tile([P, 2048], BF16, name="sq%d" % i, align_bytes=64) for i in range(NSQ)]
+        tmp = [keep.tile([P, 1024], BF16, name="tmp%d" % i) for i in range(NTMP)]
+        cd = [keep.tile([P, CHUNK], U32, name="cd%d" % i, align_bytes=64) for i in range(NCD)]
+        sc = [keep.tile([P, CHUNK], U8, name="sc%d" % i, align_bytes=64) for i in range(NCD)]
+        rt = [keep.tile([P, 4, CHUNK], F32, name="rt%d" % i) for i in range(NRT)]
+        ot = [keep.tile([P, 4, CH], F32, name="ot%d" % i) for i in range(NO)]
+
+        xb = [psum.tile([P, 512], F32, name="xb%d" % i) for i in range(2)]
+        mb = [psum.tile([P, 512], F32, name="mb%d" % i) for i in range(NM)]
+        rb = [psum.tile([P, 512], F32, name="rb%d" % i) for i in range(NR)]
+
+        xv = x.rearrange("(c p r) j -> c p r j", p=P, r=4)
+        ov = out.rearrange("(c p r) i -> c p r i", p=P, r=4)
+        gv = gamma.rearrange("(m p) j -> p m j", p=P)
+
+        nc.scalar.dma_start(out=bet[:], in_=beta.rearrange("(m p) -> m p", p=P))
+        nc.sync.dma_start(out=gam[:, 0:2, :], in_=gv[:, 0:2, :])
+        nc.sync.dma_start(out=xs[0][:, 0:2, :], in_=xv[0, :, 0:2, :])
+        nc.sync.dma_start(out=gam[:, 2:4, :], in_=gv[:, 2:4, :])
+        nc.sync.dma_start(out=xs[0][:, 2:4, :], in_=xv[0, :, 2:4, :])
+        for c in range(1, NCH):
+            nc.sync.dma_start(out=xs[c][:], in_=xv[c, :, :, :])
+
+        masks.make_identity(nc, ident[:])
+        nc.vector.memset(warm[:], 1.0)
+        nc.scalar.activation(out=warm2[:], in_=warm[:], func=ACT.Abs_reciprocal_sqrt)
+        nc.vector.memset(bz[:], 0.0)
+        nc.vector.tensor_copy(out=bz[0:4, :], in_=bet[:])
+        nc.tensor.transpose(rb[0][:, 0:P], bz[:], ident[:])
+        nc.vector.tensor_scalar_max(out=b1[:], in0=rb[0][:, 0:4], scalar1=BETA_BOUND)
+        nc.vector.tensor_tensor(out=b2[:], in0=b1[:], in1=b1[:], op=ALU.mult)
+        nc.vector.tensor_scalar_add(out=b_sb[:], in0=b2[:], scalar1=-PEDESTAL)
+
+        def words_to_bank(bank, src, half):
+            for u in range(2):
+                col = u * 256 + half * P
+                nc.tensor.transpose(bank[:, col:col + P], src.bitcast(F32)[:, u:2 * P:2], ident[:])
+
+        def bank_words(bank):
+            return bank[:].rearrange("p (u n) -> p n u", u=2)
+
+        def grouped_words(dst):
+            return dst.bitcast(F32).rearrange("p (n u) -> p n u", u=2)
+
+        def g_turn(hb):
+            for mm in range(2):
+                words_to_bank(mb[hb], gam[:, 2 * hb + mm, :], mm)
+            nc.scalar.copy(out=grouped_words(gw[hb][:]), in_=bank_words(mb[hb]))
+
+        def g_chain(hb, step):
+            cols = slice(hb * 1024, (hb + 1) * 1024)
+            wcols = slice(hb * 256, (hb + 1) * 256)
+            if step == 0:
+                nc.vector.scalar_tensor_tensor(out=g2[hb][:], in0=gw[hb][:], scalar=0.0, in1=gw[hb][:],
+                                               op0=ALU.max, op1=ALU.mult)
+            elif step == 1:
+                nc.vector.tensor_scalar(out=gq[:, cols], in0=g2[hb][:], scalar1=PEDESTAL, scalar2=-PEDESTAL,
+                                        op0=ALU.max, op1=ALU.add)
+            else:
+                nc.vector.quantize_mx(out=g_cd[:, wcols].bitcast(FP8X4), scales=g_sc[:, wcols], in_=gq[:, cols])
+
+        def ok(c):
+            return 0 <= c < NCH
+
+        def xt(c, h):
+            if ok(c):
+                for rr in range(2):
+                    words_to_bank(xb[h], xs[c][:, 2 * h + rr, :], rr)
+
+        def sq_dst(c, h):
+            return sq[c % NSQ][:, h * 1024:(h + 1) * 1024]
+
+        def sq_scalar(c, h):
+            nc.scalar.activation(
+                out=sq_dst(c, h).rearrange("p (n u e) -> p n u e", u=2, e=2),
+                in_=xb[h][:].bitcast(BF16).rearrange("p (u n e) -> p n u e", u=2, e=2),
+                func=ACT.Square)
+
+        def sq_words(c, h):
+            nc.vector.tensor_copy(out=grouped_words(tmp[(2 * c + h) % NTMP][:]), in_=bank_words(xb[h]))
+
+        def sq_mul(c, h, eng):
+            t = tmp[(2 * c + h) % NTMP]
+            eng.tensor_tensor(out=sq_dst(c, h), in0=t[:], in1=t[:], op=ALU.mult)
+
+        def quant(c):
+            if ok(c):
+                nc.vector.quantize_mx(out=cd[c % NCD][:].bitcast(FP8X4), scales=sc[c % NCD][:], in_=sq[c % NSQ][:])
+
+        def mx(c, m):
+            if ok(c):
+                cols = slice(m * P, (m + 1) * P)
+                nc.tensor.matmul_mx(out=mb[(4 * c + m) % NM][:],
+                                    lhsT=g_cd[:, cols].bitcast(FP8X4), lhsT_scale=g_sc[:, cols],
+                                    rhs=cd[c % NCD][:].bitcast(FP8X4), rhs_scale=sc[c % NCD][:],
+                                    start=True, stop=True)
+
+        def ars(c, m):
+            if ok(c):
+                nc.scalar.activation(out=rt[c % NRT][:, m, :], in_=mb[(4 * c + m) % NM][:],
+                                     func=ACT.Abs_reciprocal_sqrt, bias=b_sb[:, m:m + 1], scale=1.0)
+
+        def rtr(c, r):
+            if ok(c):
+                bank = rb[(4 * c + r) % NR]
+                for m in range(4):
+                    nc.tensor.transpose(bank[:, m * P:(m + 1) * P], rt[c % NRT][:, m, r * P:(r + 1) * P], ident[:])
+
+        def mul(c, r):
+            if ok(c):
+                nc.vector.tensor_tensor(out=ot[c % NO][:, r, :], in0=rb[(4 * c + r) % NR][:], in1=xs[c][:, r, :],
+                                        op=ALU.mult)
+
+        def store(c, r0, r1):
+            if ok(c):
+                nc.sync.dma_start(out=ov[c, :, r0:r1, :], in_=ot[c % NO][:, r0:r1, :])
+
+        def mul_store(c, r):
+            mul(c, r)
+            if c == NCH - 1:
+                store(c, r, r + 1)
+            elif r % 2 == 1:
+                store(c, r - 1, r + 1)
+
+        g_turn(0)
+        g_chain(0, 0)
+        g_chain(0, 1)
+        g_chain(0, 2)
+        pending = []
+        for k in range(-PL, NCH + 1):
+            c = k + 3 if k <= 0 else k + 4
+            mx(k, 0)
+            mx(k, 1)
+            xt(c, 0)
+            rtr(k - 1, 0)
+            rtr(k - 1, 1)
+            for (pc, ph) in pending:
+                sq_scalar(pc, ph)
+            pending = []
+            ars(k, 0)
+            ars(k, 1)
+            mul_store(k - 1, 0)
+            mul_store(k - 1, 1)
+            if k == -PL + 1:
+                g_chain(1, 0)
+            e0 = "G" if c >= HEAD else head_engine(c, 0)
+            if ok(c) and e0 == "S":
+                sq_scalar(c, 0)
+            if ok(c) and e0 != "S":
+                sq_words(c, 0)
+            if ok(c) and e0 == "V":
+                sq_mul(c, 0, nc.vector)
+            quant(k + QL)
+            if ok(c) and e0 == "G":
+                sq_mul(c, 0, nc.gpsimd)
+            if k == -PL:
+                g_turn(1)
+            if k == -PL + 1:
+                g_chain(1, 1)
+                g_chain(1, 2)
+            mx(k, 2)
+            mx(k, 3)
+            xt(c, 1)
+            rtr(k - 1, 2)
+            rtr(k - 1, 3)
+            ars(k, 2)
+            ars(k, 3)
+            mul_store(k - 1, 2)
+            mul_store(k - 1, 3)
+            e1 = "S" if c >= HEAD else head_engine(c, 1)
+            if ok(c) and e1 == "S":
+                pending.append((c, 1))
+            if ok(c) and e1 == "V":
+                sq_words(c, 1)
+                sq_mul(c, 1, nc.vector)
+            if k == 0:
+                xt(4, 0)
+                sq_words(4, 0)
+                sq_mul(4, 0, nc.gpsimd)
+                xt(4, 1)
+                pending.append((4, 1))

@@ -19,26 +19,14 @@ NCH = N_ROWS // CHUNK
 FLOPS = 2 * N_ROWS * CH * CH
 
 PEDESTAL = 2.0 ** -36
+GAMMA_BOUND = 2.0 ** -18
 BETA_BOUND = (1e-6 + PEDESTAL) ** 0.5
+RUN = 16
 
-PL = 3
-QL = 2
-NM = 3
-NR = 3
-NSQ = 6
-NCD = 4
-NRT = 3
+NSQ = 3
+NCD = 3
+NRT = 2
 NO = 4
-NTMP = 3
-
-
-HEAD = 4
-
-
-def head_engine(c, h):
-    if h == 1 and c != 1:
-        return "V"
-    return "S"
 
 
 def tile_gdn_t_kernel(tc, x, beta, gamma, out):
@@ -52,27 +40,26 @@ def tile_gdn_t_kernel(tc, x, beta, gamma, out):
         warm = keep.tile([P, 1], F32, name="warm")
         warm2 = keep.tile([P, 1], F32, name="warm2")
         gam = keep.tile([P, 4, CH], BF16, name="gam")
+        gmax = keep.tile([P, 2, CH], BF16, name="gmax")
         bet = keep.tile([4, P], BF16, name="bet")
         bz = keep.tile([P, P], F32, name="bz")
         b1 = keep.tile([P, 4], F32, name="b1")
         b2 = keep.tile([P, 4], F32, name="b2")
         b_sb = keep.tile([P, 4], F32, name="b_sb")
-        gw = [keep.tile([P, 1024], BF16, name="gw%d" % i) for i in range(2)]
         g2 = [keep.tile([P, 1024], F32, name="g2%d" % i) for i in range(2)]
         gq = keep.tile([P, 2048], BF16, name="gq", align_bytes=64)
         g_cd = keep.tile([P, CH], U32, name="g_cd", align_bytes=64)
         g_sc = keep.tile([P, CH], U8, name="g_sc", align_bytes=64)
         xs = [keep.tile([P, 4, CH], BF16, name="x%d" % c) for c in range(NCH)]
         sq = [keep.tile([P, 2048], BF16, name="sq%d" % i, align_bytes=64) for i in range(NSQ)]
-        tmp = [keep.tile([P, 1024], BF16, name="tmp%d" % i) for i in range(NTMP)]
         cd = [keep.tile([P, CHUNK], U32, name="cd%d" % i, align_bytes=64) for i in range(NCD)]
         sc = [keep.tile([P, CHUNK], U8, name="sc%d" % i, align_bytes=64) for i in range(NCD)]
         rt = [keep.tile([P, 4, CHUNK], F32, name="rt%d" % i) for i in range(NRT)]
         ot = [keep.tile([P, 4, CH], F32, name="ot%d" % i) for i in range(NO)]
 
-        xb = [psum.tile([P, 512], F32, name="xb%d" % i) for i in range(2)]
-        mb = [psum.tile([P, 512], F32, name="mb%d" % i) for i in range(NM)]
-        rb = [psum.tile([P, 512], F32, name="rb%d" % i) for i in range(NR)]
+        xb = [psum.tile([P, 512], F32, name="xb%d" % i) for i in range(1)]
+        mb = [psum.tile([P, 512], F32, name="mb%d" % i) for i in range(4)]
+        rb = [psum.tile([P, 512], F32, name="rb%d" % i) for i in range(3)]
 
         xv = x.rearrange("(c p r) j -> c p r j", p=P, r=4)
         ov = out.rearrange("(c p r) i -> c p r i", p=P, r=4)
@@ -90,16 +77,35 @@ def tile_gdn_t_kernel(tc, x, beta, gamma, out):
         nc.vector.memset(warm[:], 1.0)
         nc.scalar.activation(out=warm2[:], in_=warm[:], func=ACT.Abs_reciprocal_sqrt)
         nc.vector.memset(bz[:], 0.0)
-        nc.vector.tensor_copy(out=bz[0:4, :], in_=bet[:])
-        nc.tensor.transpose(rb[0][:, 0:P], bz[:], ident[:])
-        nc.vector.tensor_scalar_max(out=b1[:], in0=rb[0][:, 0:4], scalar1=BETA_BOUND)
-        nc.vector.tensor_tensor(out=b2[:], in0=b1[:], in1=b1[:], op=ALU.mult)
-        nc.vector.tensor_scalar_add(out=b_sb[:], in0=b2[:], scalar1=-PEDESTAL)
 
-        def words_to_bank(bank, src, half):
-            for u in range(2):
-                col = u * 256 + half * P
-                nc.tensor.transpose(bank[:, col:col + P], src.bitcast(F32)[:, u:2 * P:2], ident[:])
+        def bias_turn():
+            nc.vector.tensor_copy(out=bz[0:4, :], in_=bet[:])
+            nc.tensor.transpose(rb[0][:, 0:P], bz[:], ident[:])
+
+        def bias_max():
+            nc.vector.tensor_scalar_max(out=b1[:], in0=rb[0][:, 0:4], scalar1=BETA_BOUND)
+
+        def bias_square():
+            nc.vector.tensor_tensor(out=b2[:], in0=b1[:], in1=b1[:], op=ALU.mult)
+
+        def bias_less():
+            nc.vector.tensor_scalar_add(out=b_sb[:], in0=b2[:], scalar1=-PEDESTAL)
+
+        def runs(pair):
+            return pair.rearrange("p r (q u s) -> p u (r q) s", u=2, s=RUN)
+
+        def flat(pair):
+            return pair.rearrange("p r j -> p (r j)")
+
+        def half(t, h):
+            return t[:, h * 1024:(h + 1) * 1024]
+
+        def turned_dst(t, h):
+            return half(t, h).rearrange("p (u a s) -> p u a s", u=2, s=RUN)
+
+        def words_to_bank(bank, nat):
+            for b in range(4):
+                nc.tensor.transpose(bank[:, b * P:(b + 1) * P], nat.bitcast(F32)[:, b * P:(b + 1) * P], ident[:])
 
         def bank_words(bank):
             return bank[:].rearrange("p (u n) -> p n u", u=2)
@@ -107,46 +113,21 @@ def tile_gdn_t_kernel(tc, x, beta, gamma, out):
         def grouped_words(dst):
             return dst.bitcast(F32).rearrange("p (n u) -> p n u", u=2)
 
-        def g_turn(hb):
-            for mm in range(2):
-                words_to_bank(mb[hb], gam[:, 2 * hb + mm, :], mm)
-            nc.scalar.copy(out=grouped_words(gw[hb][:]), in_=bank_words(mb[hb]))
-
-        def g_chain(hb, step):
-            cols = slice(hb * 1024, (hb + 1) * 1024)
-            wcols = slice(hb * 256, (hb + 1) * 256)
-            if step == 0:
-                nc.vector.scalar_tensor_tensor(out=g2[hb][:], in0=gw[hb][:], scalar=0.0, in1=gw[hb][:],
-                                               op0=ALU.max, op1=ALU.mult)
-            elif step == 1:
-                nc.vector.tensor_scalar(out=gq[:, cols], in0=g2[hb][:], scalar1=PEDESTAL, scalar2=-PEDESTAL,
-                                        op0=ALU.max, op1=ALU.add)
-            else:
-                nc.vector.quantize_mx(out=g_cd[:, wcols].bitcast(FP8X4), scales=g_sc[:, wcols], in_=gq[:, cols])
-
         def ok(c):
             return 0 <= c < NCH
 
-        def xt(c, h):
+        def sq_on(c, h, eng):
             if ok(c):
-                for rr in range(2):
-                    words_to_bank(xb[h], xs[c][:, 2 * h + rr, :], rr)
+                src = runs(xs[c][:, 2 * h:2 * h + 2, :])
+                eng.tensor_tensor(out=turned_dst(sq[c % NSQ], h), in0=src, in1=src, op=ALU.mult)
 
-        def sq_dst(c, h):
-            return sq[c % NSQ][:, h * 1024:(h + 1) * 1024]
+        def xt(c, h, bank):
+            if ok(c):
+                words_to_bank(bank, half(sq[c % NSQ], h))
 
-        def sq_scalar(c, h):
-            nc.scalar.activation(
-                out=sq_dst(c, h).rearrange("p (n u e) -> p n u e", u=2, e=2),
-                in_=xb[h][:].bitcast(BF16).rearrange("p (u n e) -> p n u e", u=2, e=2),
-                func=ACT.Square)
-
-        def sq_words(c, h):
-            nc.vector.tensor_copy(out=grouped_words(tmp[(2 * c + h) % NTMP][:]), in_=bank_words(xb[h]))
-
-        def sq_mul(c, h, eng):
-            t = tmp[(2 * c + h) % NTMP]
-            eng.tensor_tensor(out=sq_dst(c, h), in0=t[:], in1=t[:], op=ALU.mult)
+        def out_words(c, h, bank):
+            if ok(c):
+                nc.scalar.copy(out=grouped_words(half(sq[c % NSQ], h)), in_=bank_words(bank))
 
         def quant(c):
             if ok(c):
@@ -155,92 +136,118 @@ def tile_gdn_t_kernel(tc, x, beta, gamma, out):
         def mx(c, m):
             if ok(c):
                 cols = slice(m * P, (m + 1) * P)
-                nc.tensor.matmul_mx(out=mb[(4 * c + m) % NM][:],
+                nc.tensor.matmul_mx(out=mb[m][:],
                                     lhsT=g_cd[:, cols].bitcast(FP8X4), lhsT_scale=g_sc[:, cols],
                                     rhs=cd[c % NCD][:].bitcast(FP8X4), rhs_scale=sc[c % NCD][:],
                                     start=True, stop=True)
 
         def ars(c, m):
             if ok(c):
-                nc.scalar.activation(out=rt[c % NRT][:, m, :], in_=mb[(4 * c + m) % NM][:],
+                nc.scalar.activation(out=rt[c % NRT][:, m, :], in_=mb[m][:],
                                      func=ACT.Abs_reciprocal_sqrt, bias=b_sb[:, m:m + 1], scale=1.0)
 
         def rtr(c, r):
             if ok(c):
-                bank = rb[(4 * c + r) % NR]
                 for m in range(4):
-                    nc.tensor.transpose(bank[:, m * P:(m + 1) * P], rt[c % NRT][:, m, r * P:(r + 1) * P], ident[:])
+                    nc.tensor.transpose(rb[(4 * c + r) % 3][:, m * P:(m + 1) * P], rt[c % NRT][:, m, r * P:(r + 1) * P], ident[:])
 
         def mul(c, r):
             if ok(c):
-                nc.vector.tensor_tensor(out=ot[c % NO][:, r, :], in0=rb[(4 * c + r) % NR][:], in1=xs[c][:, r, :],
+                nc.vector.tensor_tensor(out=ot[c % NO][:, r, :], in0=rb[(4 * c + r) % 3][:], in1=xs[c][:, r, :],
                                         op=ALU.mult)
+                if c == NCH - 1:
+                    store(c, r, r + 1)
+                elif r % 2 == 1:
+                    store(c, r - 1, r + 1)
 
         def store(c, r0, r1):
-            if ok(c):
-                nc.sync.dma_start(out=ov[c, :, r0:r1, :], in_=ot[c % NO][:, r0:r1, :])
+            nc.sync.dma_start(out=ov[c, :, r0:r1, :], in_=ot[c % NO][:, r0:r1, :])
 
-        def mul_store(c, r):
-            mul(c, r)
-            if c == NCH - 1:
-                store(c, r, r + 1)
-            elif r % 2 == 1:
-                store(c, r - 1, r + 1)
+        def g_max(h):
+            nc.vector.tensor_scalar_max(out=turned_dst(gq, h), in0=runs(gam[:, 2 * h:2 * h + 2, :]),
+                                        scalar1=GAMMA_BOUND)
 
-        g_turn(0)
-        g_chain(0, 0)
-        g_chain(0, 1)
-        g_chain(0, 2)
-        pending = []
-        for k in range(-PL, NCH + 1):
-            c = k + 3 if k <= 0 else k + 4
-            mx(k, 0)
-            mx(k, 1)
-            xt(c, 0)
+        def g_square(h):
+            nc.scalar.activation(
+                out=g2[h][:].rearrange("p (n u e) -> p n u e", u=2, e=2),
+                in_=mb[2 + h][:].bitcast(BF16).rearrange("p (u n e) -> p n u e", u=2, e=2),
+                func=ACT.Square)
+
+        def g_less(h):
+            nc.vector.tensor_scalar_add(out=half(gq, h), in0=g2[h][:], scalar1=-PEDESTAL)
+
+        def g_quant(h):
+            wcols = slice(h * 256, (h + 1) * 256)
+            nc.vector.quantize_mx(out=g_cd[:, wcols].bitcast(FP8X4), scales=g_sc[:, wcols], in_=half(gq, h))
+
+        bias_turn()
+        g_max(0)
+        bias_max()
+        sq_on(0, 0, nc.vector)
+        g_max(1)
+        bias_square()
+        words_to_bank(mb[2], half(gq, 0))
+        xt(0, 0, mb[0])
+        g_square(0)
+        out_words(0, 0, mb[0])
+        sq_on(0, 1, nc.vector)
+        bias_less()
+        xt(0, 1, xb[0])
+        out_words(0, 1, xb[0])
+        words_to_bank(mb[3], half(gq, 1))
+        g_square(1)
+        g_less(0)
+        g_quant(0)
+        quant(0)
+        sq_on(1, 0, nc.vector)
+        mx(0, 0)
+        mx(0, 1)
+        xt(1, 0, rb[1])
+        ars(0, 0)
+        ars(0, 1)
+        out_words(1, 0, rb[1])
+        g_less(1)
+        g_quant(1)
+        sq_on(1, 1, nc.vector)
+        mx(0, 2)
+        mx(0, 3)
+        xt(1, 1, rb[2])
+        ars(0, 2)
+        ars(0, 3)
+        out_words(1, 1, rb[2])
+        sq_on(2, 0, nc.vector)
+        sq_on(2, 1, nc.vector)
+        xt(2, 0, mb[0])
+        xt(2, 1, xb[0])
+        out_words(2, 0, mb[0])
+        out_words(2, 1, xb[0])
+        sq_on(3, 0, nc.vector)
+        sq_on(3, 1, nc.vector)
+        quant(1)
+        sq_on(4, 0, nc.vector)
+        sq_on(4, 1, nc.vector)
+        for k in range(1, NCH + 1):
+            for m in range(4):
+                mx(k, m)
             rtr(k - 1, 0)
-            rtr(k - 1, 1)
-            for (pc, ph) in pending:
-                sq_scalar(pc, ph)
-            pending = []
             ars(k, 0)
-            ars(k, 1)
-            mul_store(k - 1, 0)
-            mul_store(k - 1, 1)
-            if k == -PL + 1:
-                g_chain(1, 0)
-            e0 = "G" if c >= HEAD else head_engine(c, 0)
-            if ok(c) and e0 == "S":
-                sq_scalar(c, 0)
-            if ok(c) and e0 != "S":
-                sq_words(c, 0)
-            if ok(c) and e0 == "V":
-                sq_mul(c, 0, nc.vector)
-            quant(k + QL)
-            if ok(c) and e0 == "G":
-                sq_mul(c, 0, nc.gpsimd)
-            if k == -PL:
-                g_turn(1)
-            if k == -PL + 1:
-                g_chain(1, 1)
-                g_chain(1, 2)
-            mx(k, 2)
-            mx(k, 3)
-            xt(c, 1)
+            xt(k + 2, 0, mb[0])
+            rtr(k - 1, 1)
             rtr(k - 1, 2)
-            rtr(k - 1, 3)
+            xt(k + 2, 1, xb[0])
+            ars(k, 1)
             ars(k, 2)
+            out_words(k + 2, 0, mb[0])
             ars(k, 3)
-            mul_store(k - 1, 2)
-            mul_store(k - 1, 3)
-            e1 = "S" if c >= HEAD else head_engine(c, 1)
-            if ok(c) and e1 == "S":
-                pending.append((c, 1))
-            if ok(c) and e1 == "V":
-                sq_words(c, 1)
-                sq_mul(c, 1, nc.vector)
-            if k == 0:
-                xt(4, 0)
-                sq_words(4, 0)
-                sq_mul(4, 0, nc.gpsimd)
-                xt(4, 1)
-                pending.append((4, 1))
+            out_words(k + 2, 1, xb[0])
+            mul(k - 1, 0)
+            if k == 1:
+                quant(2)
+                sq_on(5, 1, nc.gpsimd)
+            rtr(k - 1, 3)
+            mul(k - 1, 1)
+            mul(k - 1, 2)
+            mul(k - 1, 3)
+            sq_on(k + 1 + NSQ, 0, nc.vector)
+            quant(k + 2)
+            sq_on(k + 2 + NSQ, 1, nc.gpsimd)

@@ -23,7 +23,7 @@ GAMMA_BOUND = 2.0 ** -18
 BETA_BOUND = (1e-6 + PEDESTAL) ** 0.5
 RUN = 16
 
-NSQ = 3
+NSQ = 4
 NCD = 3
 NRT = 2
 NO = 4
@@ -57,8 +57,8 @@ def tile_gdn_t_kernel(tc, x, beta, gamma, out):
         rt = [keep.tile([P, 4, CHUNK], F32, name="rt%d" % i) for i in range(NRT)]
         ot = [keep.tile([P, 4, CH], F32, name="ot%d" % i) for i in range(NO)]
 
-        xb = [psum.tile([P, 512], F32, name="xb%d" % i) for i in range(1)]
-        mb = [psum.tile([P, 512], F32, name="mb%d" % i) for i in range(4)]
+        xb = [psum.tile([P, 512], F32, name="xb%d" % i) for i in range(2)]
+        mb = [psum.tile([P, 512], F32, name="mb%d" % i) for i in range(3)]
         rb = [psum.tile([P, 512], F32, name="rb%d" % i) for i in range(3)]
 
         xv = x.rearrange("(c p r) j -> c p r j", p=P, r=4)
@@ -136,14 +136,14 @@ def tile_gdn_t_kernel(tc, x, beta, gamma, out):
         def mx(c, m):
             if ok(c):
                 cols = slice(m * P, (m + 1) * P)
-                nc.tensor.matmul_mx(out=mb[m][:],
+                nc.tensor.matmul_mx(out=mb[(4 * c + m) % 3][:],
                                     lhsT=g_cd[:, cols].bitcast(FP8X4), lhsT_scale=g_sc[:, cols],
                                     rhs=cd[c % NCD][:].bitcast(FP8X4), rhs_scale=sc[c % NCD][:],
                                     start=True, stop=True)
 
         def ars(c, m):
             if ok(c):
-                nc.scalar.activation(out=rt[c % NRT][:, m, :], in_=mb[m][:],
+                nc.scalar.activation(out=rt[c % NRT][:, m, :], in_=mb[(4 * c + m) % 3][:],
                                      func=ACT.Abs_reciprocal_sqrt, bias=b_sb[:, m:m + 1], scale=1.0)
 
         def rtr(c, r):
@@ -170,7 +170,7 @@ def tile_gdn_t_kernel(tc, x, beta, gamma, out):
         def g_square(h):
             nc.scalar.activation(
                 out=g2[h][:].rearrange("p (n u e) -> p n u e", u=2, e=2),
-                in_=mb[2 + h][:].bitcast(BF16).rearrange("p (u n e) -> p n u e", u=2, e=2),
+                in_=mb[1 + h][:].bitcast(BF16).rearrange("p (u n e) -> p n u e", u=2, e=2),
                 func=ACT.Square)
 
         def g_less(h):
@@ -186,15 +186,15 @@ def tile_gdn_t_kernel(tc, x, beta, gamma, out):
         sq_on(0, 0, nc.vector)
         g_max(1)
         bias_square()
-        words_to_bank(mb[2], half(gq, 0))
-        xt(0, 0, mb[0])
+        words_to_bank(mb[1], half(gq, 0))
+        xt(0, 0, xb[0])
         g_square(0)
-        out_words(0, 0, mb[0])
+        out_words(0, 0, xb[0])
         sq_on(0, 1, nc.vector)
         bias_less()
-        xt(0, 1, xb[0])
-        out_words(0, 1, xb[0])
-        words_to_bank(mb[3], half(gq, 1))
+        xt(0, 1, xb[1])
+        out_words(0, 1, xb[1])
+        words_to_bank(mb[2], half(gq, 1))
         g_square(1)
         g_less(0)
         g_quant(0)
@@ -202,52 +202,61 @@ def tile_gdn_t_kernel(tc, x, beta, gamma, out):
         sq_on(1, 0, nc.vector)
         mx(0, 0)
         mx(0, 1)
-        xt(1, 0, rb[1])
+        xt(1, 0, xb[0])
         ars(0, 0)
         ars(0, 1)
-        out_words(1, 0, rb[1])
+        out_words(1, 0, xb[0])
         g_less(1)
         g_quant(1)
         sq_on(1, 1, nc.vector)
         mx(0, 2)
         mx(0, 3)
-        xt(1, 1, rb[2])
+        xt(1, 1, xb[1])
         ars(0, 2)
         ars(0, 3)
-        out_words(1, 1, rb[2])
+        out_words(1, 1, xb[1])
         sq_on(2, 0, nc.vector)
         sq_on(2, 1, nc.vector)
-        xt(2, 0, mb[0])
-        xt(2, 1, xb[0])
-        out_words(2, 0, mb[0])
-        out_words(2, 1, xb[0])
+        xt(2, 0, xb[0])
+        xt(2, 1, xb[1])
+        out_words(2, 0, xb[0])
+        out_words(2, 1, xb[1])
         sq_on(3, 0, nc.vector)
-        sq_on(3, 1, nc.vector)
         quant(1)
+        sq_on(3, 1, nc.vector)
+        xt(3, 0, xb[0])
+        xt(3, 1, xb[1])
+        out_words(3, 0, xb[0])
         sq_on(4, 0, nc.vector)
         sq_on(4, 1, nc.vector)
+        sq_on(5, 0, nc.vector)
+        sq_on(5, 1, nc.vector)
         for k in range(1, NCH + 1):
-            for m in range(4):
-                mx(k, m)
-            rtr(k - 1, 0)
+            mx(k, 0)
+            mx(k, 1)
             ars(k, 0)
-            xt(k + 2, 0, mb[0])
-            rtr(k - 1, 1)
-            rtr(k - 1, 2)
-            xt(k + 2, 1, xb[0])
             ars(k, 1)
-            ars(k, 2)
-            out_words(k + 2, 0, mb[0])
-            ars(k, 3)
-            out_words(k + 2, 1, xb[0])
+            out_words(k + 2, 1, xb[1])
+            rtr(k - 1, 0)
+            rtr(k - 1, 1)
+            xt(k + 3, 0, xb[0])
             mul(k - 1, 0)
-            if k == 1:
-                quant(2)
-                sq_on(5, 1, nc.gpsimd)
-            rtr(k - 1, 3)
             mul(k - 1, 1)
-            mul(k - 1, 2)
-            mul(k - 1, 3)
-            sq_on(k + 1 + NSQ, 0, nc.vector)
+            if k > 1:
+                sq_on(k + 1 + NSQ, 0, nc.vector)
+            else:
+                quant(2)
+                sq_on(6, 0, nc.vector)
+                sq_on(6, 1, nc.vector)
             quant(k + 2)
             sq_on(k + 2 + NSQ, 1, nc.gpsimd)
+            mx(k, 2)
+            mx(k, 3)
+            ars(k, 2)
+            ars(k, 3)
+            out_words(k + 3, 0, xb[0])
+            rtr(k - 1, 2)
+            rtr(k - 1, 3)
+            xt(k + 3, 1, xb[1])
+            mul(k - 1, 2)
+            mul(k - 1, 3)

@@ -23,7 +23,7 @@ GAMMA_BOUND = 2.0 ** -18
 BETA_BOUND = (1e-6 + PEDESTAL) ** 0.5
 RUN = 16
 
-NSQ = 4
+NSQ = 5
 NCD = 3
 NRT = 2
 NO = 4
@@ -120,6 +120,12 @@ def tile_gdn_t_kernel(tc, x, beta, gamma, out):
             if ok(c):
                 src = runs(xs[c][:, 2 * h:2 * h + 2, :])
                 eng.tensor_tensor(out=turned_dst(sq[c % NSQ], h), in0=src, in1=src, op=ALU.mult)
+
+        def sq_tile(c, r, eng):
+            if ok(c):
+                src = runs(xs[c][:, r:r + 1, :])
+                dst = half(sq[c % NSQ], r // 2).rearrange("p (u t q s) -> p t u q s", u=2, t=2, s=RUN)[:, r % 2]
+                eng.tensor_tensor(out=dst, in0=src, in1=src, op=ALU.mult)
 
         def xt(c, h, bank):
             if ok(c):
@@ -231,6 +237,9 @@ def tile_gdn_t_kernel(tc, x, beta, gamma, out):
         sq_on(4, 1, nc.vector)
         sq_on(5, 0, nc.vector)
         sq_on(5, 1, nc.vector)
+        sq_on(6, 0, nc.vector)
+        sq_tile(6, 2, nc.vector)
+        sq_tile(6, 3, nc.gpsimd)
         for k in range(1, NCH + 1):
             mx(k, 0)
             mx(k, 1)
@@ -242,14 +251,12 @@ def tile_gdn_t_kernel(tc, x, beta, gamma, out):
             xt(k + 3, 0, xb[0])
             mul(k - 1, 0)
             mul(k - 1, 1)
-            if k > 1:
-                sq_on(k + 1 + NSQ, 0, nc.vector)
-            else:
+            if k == 1:
                 quant(2)
-                sq_on(6, 0, nc.vector)
-                sq_on(6, 1, nc.vector)
             quant(k + 2)
-            sq_on(k + 2 + NSQ, 1, nc.gpsimd)
+            sq_on(k + 1 + NSQ, 0, nc.vector)
+            sq_tile(k + 1 + NSQ, 2, nc.vector)
+            sq_tile(k + 1 + NSQ, 3, nc.gpsimd)
             mx(k, 2)
             mx(k, 3)
             ars(k, 2)

@@ -23,7 +23,7 @@ GAMMA_BOUND = 2.0 ** -18
 BETA_BOUND = (1e-6 + PEDESTAL) ** 0.5
 RUN = 16
 
-NSQ = 5
+NSQ = 4
 NCD = 3
 NRT = 2
 NO = 4
@@ -57,8 +57,8 @@ def tile_gdn_t_kernel(tc, x, beta, gamma, out):
         rt = [keep.tile([P, 4, CHUNK], F32, name="rt%d" % i) for i in range(NRT)]
         ot = [keep.tile([P, 4, CH], F32, name="ot%d" % i) for i in range(NO)]
 
-        xb = [psum.tile([P, 512], F32, name="xb%d" % i) for i in range(2)]
-        mb = [psum.tile([P, 512], F32, name="mb%d" % i) for i in range(3)]
+        xb = [psum.tile([P, 512], F32, name="xb%d" % i) for i in range(1)]
+        mb = [psum.tile([P, 512], F32, name="mb%d" % i) for i in range(4)]
         rb = [psum.tile([P, 512], F32, name="rb%d" % i) for i in range(3)]
 
         xv = x.rearrange("(c p r) j -> c p r j", p=P, r=4)
@@ -142,14 +142,14 @@ def tile_gdn_t_kernel(tc, x, beta, gamma, out):
         def mx(c, m):
             if ok(c):
                 cols = slice(m * P, (m + 1) * P)
-                nc.tensor.matmul_mx(out=mb[(4 * c + m) % 3][:],
+                nc.tensor.matmul_mx(out=mb[m][:],
                                     lhsT=g_cd[:, cols].bitcast(FP8X4), lhsT_scale=g_sc[:, cols],
                                     rhs=cd[c % NCD][:].bitcast(FP8X4), rhs_scale=sc[c % NCD][:],
                                     start=True, stop=True)
 
         def ars(c, m):
             if ok(c):
-                nc.scalar.activation(out=rt[c % NRT][:, m, :], in_=mb[(4 * c + m) % 3][:],
+                nc.scalar.activation(out=rt[c % NRT][:, m, :], in_=mb[m][:],
                                      func=ACT.Abs_reciprocal_sqrt, bias=b_sb[:, m:m + 1], scale=1.0)
 
         def rtr(c, r):
@@ -176,7 +176,7 @@ def tile_gdn_t_kernel(tc, x, beta, gamma, out):
         def g_square(h):
             nc.scalar.activation(
                 out=g2[h][:].rearrange("p (n u e) -> p n u e", u=2, e=2),
-                in_=mb[1 + h][:].bitcast(BF16).rearrange("p (u n e) -> p n u e", u=2, e=2),
+                in_=mb[2 + h][:].bitcast(BF16).rearrange("p (u n e) -> p n u e", u=2, e=2),
                 func=ACT.Square)
 
         def g_less(h):
@@ -192,15 +192,15 @@ def tile_gdn_t_kernel(tc, x, beta, gamma, out):
         sq_on(0, 0, nc.vector)
         g_max(1)
         bias_square()
-        words_to_bank(mb[1], half(gq, 0))
-        xt(0, 0, xb[0])
+        words_to_bank(mb[2], half(gq, 0))
+        xt(0, 0, mb[0])
         g_square(0)
-        out_words(0, 0, xb[0])
+        out_words(0, 0, mb[0])
         sq_on(0, 1, nc.vector)
         bias_less()
-        xt(0, 1, xb[1])
-        out_words(0, 1, xb[1])
-        words_to_bank(mb[2], half(gq, 1))
+        xt(0, 1, xb[0])
+        out_words(0, 1, xb[0])
+        words_to_bank(mb[3], half(gq, 1))
         g_square(1)
         g_less(0)
         g_quant(0)
@@ -208,62 +208,54 @@ def tile_gdn_t_kernel(tc, x, beta, gamma, out):
         sq_on(1, 0, nc.vector)
         mx(0, 0)
         mx(0, 1)
-        xt(1, 0, xb[0])
+        xt(1, 0, rb[1])
         ars(0, 0)
         ars(0, 1)
-        out_words(1, 0, xb[0])
+        out_words(1, 0, rb[1])
         g_less(1)
         g_quant(1)
         sq_on(1, 1, nc.vector)
         mx(0, 2)
         mx(0, 3)
-        xt(1, 1, xb[1])
+        xt(1, 1, rb[2])
         ars(0, 2)
         ars(0, 3)
-        out_words(1, 1, xb[1])
+        out_words(1, 1, rb[2])
         sq_on(2, 0, nc.vector)
         sq_on(2, 1, nc.vector)
-        xt(2, 0, xb[0])
-        xt(2, 1, xb[1])
-        out_words(2, 0, xb[0])
-        out_words(2, 1, xb[1])
+        xt(2, 0, mb[0])
+        xt(2, 1, xb[0])
+        out_words(2, 0, mb[0])
+        out_words(2, 1, xb[0])
         sq_on(3, 0, nc.vector)
-        quant(1)
         sq_on(3, 1, nc.vector)
-        xt(3, 0, xb[0])
-        xt(3, 1, xb[1])
-        out_words(3, 0, xb[0])
+        quant(1)
         sq_on(4, 0, nc.vector)
         sq_on(4, 1, nc.vector)
         sq_on(5, 0, nc.vector)
         sq_on(5, 1, nc.vector)
-        sq_on(6, 0, nc.vector)
-        sq_tile(6, 2, nc.vector)
-        sq_tile(6, 3, nc.gpsimd)
         for k in range(1, NCH + 1):
-            mx(k, 0)
-            mx(k, 1)
-            ars(k, 0)
-            ars(k, 1)
-            out_words(k + 2, 1, xb[1])
+            for m in range(4):
+                mx(k, m)
             rtr(k - 1, 0)
+            ars(k, 0)
+            xt(k + 2, 0, mb[0])
             rtr(k - 1, 1)
-            xt(k + 3, 0, xb[0])
+            rtr(k - 1, 2)
+            xt(k + 2, 1, xb[0])
+            ars(k, 1)
+            ars(k, 2)
+            out_words(k + 2, 0, mb[0])
+            ars(k, 3)
+            out_words(k + 2, 1, xb[0])
             mul(k - 1, 0)
-            mul(k - 1, 1)
             if k == 1:
                 quant(2)
-            quant(k + 2)
+            rtr(k - 1, 3)
+            mul(k - 1, 1)
+            mul(k - 1, 2)
+            mul(k - 1, 3)
             sq_on(k + 1 + NSQ, 0, nc.vector)
             sq_tile(k + 1 + NSQ, 2, nc.vector)
             sq_tile(k + 1 + NSQ, 3, nc.gpsimd)
-            mx(k, 2)
-            mx(k, 3)
-            ars(k, 2)
-            ars(k, 3)
-            out_words(k + 3, 0, xb[0])
-            rtr(k - 1, 2)
-            rtr(k - 1, 3)
-            xt(k + 3, 1, xb[1])
-            mul(k - 1, 2)
-            mul(k - 1, 3)
+            quant(k + 2)

@@ -23,9 +23,9 @@ GAMMA_BOUND = 2.0 ** -18
 BETA_BOUND = (1e-6 + PEDESTAL) ** 0.5
 RUN = 16
 
-NSQ = 4
+NSQ = 5
 NCD = 3
-NRT = 2
+NRT = 3
 NO = 4
 
 
@@ -40,7 +40,6 @@ def tile_gdn_t_kernel(tc, x, beta, gamma, out):
         warm = keep.tile([P, 1], F32, name="warm")
         warm2 = keep.tile([P, 1], F32, name="warm2")
         gam = keep.tile([P, 4, CH], BF16, name="gam")
-        gmax = keep.tile([P, 2, CH], BF16, name="gmax")
         bet = keep.tile([4, P], BF16, name="bet")
         bz = keep.tile([P, P], F32, name="bz")
         b1 = keep.tile([P, 4], F32, name="b1")
@@ -91,21 +90,22 @@ def tile_gdn_t_kernel(tc, x, beta, gamma, out):
         def bias_less():
             nc.vector.tensor_scalar_add(out=b_sb[:], in0=b2[:], scalar1=-PEDESTAL)
 
-        def runs(pair):
-            return pair.rearrange("p r (q u s) -> p u (r q) s", u=2, s=RUN)
-
         def flat(pair):
             return pair.rearrange("p r j -> p (r j)")
 
         def half(t, h):
             return t[:, h * 1024:(h + 1) * 1024]
 
-        def turned_dst(t, h):
-            return half(t, h).rearrange("p (u a s) -> p u a s", u=2, s=RUN)
-
-        def words_to_bank(bank, nat):
+        def turn_near(bank, rows):
             for b in range(4):
-                nc.tensor.transpose(bank[:, b * P:(b + 1) * P], nat.bitcast(F32)[:, b * P:(b + 1) * P], ident[:])
+                nc.tensor.transpose(bank[:, b * P:(b + 1) * P], rows.bitcast(F32)[:, b * P:(b + 1) * P], ident[:])
+
+        def turn(bank, rows):
+            words = rows.bitcast(F32)
+            for u in range(2):
+                for t in range(2):
+                    nc.tensor.transpose(bank[:, (2 * u + t) * P:(2 * u + t + 1) * P],
+                                        words[:, 256 * t + u:256 * (t + 1):2], ident[:])
 
         def bank_words(bank):
             return bank[:].rearrange("p (u n) -> p n u", u=2)
@@ -113,27 +113,41 @@ def tile_gdn_t_kernel(tc, x, beta, gamma, out):
         def grouped_words(dst):
             return dst.bitcast(F32).rearrange("p (n u) -> p n u", u=2)
 
+        def grouped(dst):
+            return dst.rearrange("p (n u e) -> p n u e", u=2, e=2)
+
+        def bank_pairs(bank):
+            return bank[:].bitcast(BF16).rearrange("p (u n e) -> p n u e", u=2, e=2)
+
         def ok(c):
             return 0 <= c < NCH
 
-        def sq_on(c, h, eng):
+        def sq_nat(c, eng):
             if ok(c):
-                src = runs(xs[c][:, 2 * h:2 * h + 2, :])
-                eng.tensor_tensor(out=turned_dst(sq[c % NSQ], h), in0=src, in1=src, op=ALU.mult)
-
-        def sq_tile(c, r, eng):
-            if ok(c):
-                src = runs(xs[c][:, r:r + 1, :])
-                dst = half(sq[c % NSQ], r // 2).rearrange("p (u t q s) -> p t u q s", u=2, t=2, s=RUN)[:, r % 2]
+                src = flat(xs[c][:, 0:2, :]).rearrange("p (w u e) -> p u w e", u=2, e=2)
+                dst = half(sq[c % NSQ], 0).rearrange("p (u w e) -> p u w e", u=2, e=2)
                 eng.tensor_tensor(out=dst, in0=src, in1=src, op=ALU.mult)
 
         def xt(c, h, bank):
             if ok(c):
-                words_to_bank(bank, half(sq[c % NSQ], h))
+                if h == 0:
+                    turn_near(bank, half(sq[c % NSQ], 0))
+                else:
+                    turn(bank, flat(xs[c][:, 2:4, :]))
 
-        def out_words(c, h, bank):
+        def xt_far(c, h, bank):
+            turn(bank, flat(xs[c][:, 2 * h:2 * h + 2, :]))
+
+        def sq_far(c, h, bank):
+            nc.scalar.activation(out=grouped(half(sq[c % NSQ], h)), in_=bank_pairs(bank), func=ACT.Square)
+
+        def words_back(c, bank):
             if ok(c):
-                nc.scalar.copy(out=grouped_words(half(sq[c % NSQ], h)), in_=bank_words(bank))
+                nc.vector.tensor_copy(out=grouped_words(half(sq[c % NSQ], 0)), in_=bank_words(bank))
+
+        def sq_turned(c, bank):
+            if ok(c):
+                nc.scalar.activation(out=grouped(half(sq[c % NSQ], 1)), in_=bank_pairs(bank), func=ACT.Square)
 
         def quant(c):
             if ok(c):
@@ -152,14 +166,16 @@ def tile_gdn_t_kernel(tc, x, beta, gamma, out):
                 nc.scalar.activation(out=rt[c % NRT][:, m, :], in_=mb[m][:],
                                      func=ACT.Abs_reciprocal_sqrt, bias=b_sb[:, m:m + 1], scale=1.0)
 
-        def rtr(c, r):
+        def rtr(j):
+            c, r = divmod(j, 4)
             if ok(c):
                 for m in range(4):
-                    nc.tensor.transpose(rb[(4 * c + r) % 3][:, m * P:(m + 1) * P], rt[c % NRT][:, m, r * P:(r + 1) * P], ident[:])
+                    nc.tensor.transpose(rb[j % 3][:, m * P:(m + 1) * P], rt[c % NRT][:, m, r * P:(r + 1) * P], ident[:])
 
-        def mul(c, r):
+        def mul(j):
+            c, r = divmod(j, 4)
             if ok(c):
-                nc.vector.tensor_tensor(out=ot[c % NO][:, r, :], in0=rb[(4 * c + r) % 3][:], in1=xs[c][:, r, :],
+                nc.vector.tensor_tensor(out=ot[c % NO][:, r, :], in0=rb[j % 3][:], in1=xs[c][:, r, :],
                                         op=ALU.mult)
                 if c == NCH - 1:
                     store(c, r, r + 1)
@@ -170,14 +186,10 @@ def tile_gdn_t_kernel(tc, x, beta, gamma, out):
             nc.sync.dma_start(out=ov[c, :, r0:r1, :], in_=ot[c % NO][:, r0:r1, :])
 
         def g_max(h):
-            nc.vector.tensor_scalar_max(out=turned_dst(gq, h), in0=runs(gam[:, 2 * h:2 * h + 2, :]),
-                                        scalar1=GAMMA_BOUND)
+            nc.vector.tensor_scalar_max(out=half(gq, h), in0=flat(gam[:, 2 * h:2 * h + 2, :]), scalar1=GAMMA_BOUND)
 
-        def g_square(h):
-            nc.scalar.activation(
-                out=g2[h][:].rearrange("p (n u e) -> p n u e", u=2, e=2),
-                in_=mb[2 + h][:].bitcast(BF16).rearrange("p (u n e) -> p n u e", u=2, e=2),
-                func=ACT.Square)
+        def g_square(h, bank):
+            nc.scalar.activation(out=grouped(g2[h][:]), in_=bank_pairs(bank), func=ACT.Square)
 
         def g_less(h):
             nc.vector.tensor_scalar_add(out=half(gq, h), in0=g2[h][:], scalar1=-PEDESTAL)
@@ -189,73 +201,83 @@ def tile_gdn_t_kernel(tc, x, beta, gamma, out):
         bias_turn()
         g_max(0)
         bias_max()
-        sq_on(0, 0, nc.vector)
+        sq_nat(0, nc.vector)
         g_max(1)
         bias_square()
-        words_to_bank(mb[2], half(gq, 0))
+        turn(mb[1], half(gq, 0))
         xt(0, 0, mb[0])
-        g_square(0)
-        out_words(0, 0, mb[0])
-        sq_on(0, 1, nc.vector)
-        bias_less()
+        g_square(0, mb[1])
         xt(0, 1, xb[0])
-        out_words(0, 1, xb[0])
-        words_to_bank(mb[3], half(gq, 1))
-        g_square(1)
+        sq_turned(0, xb[0])
+        words_back(0, mb[0])
+        bias_less()
+        turn(mb[2], half(gq, 1))
+        xt_far(1, 0, mb[3])
+        g_square(1, mb[2])
         g_less(0)
         g_quant(0)
         quant(0)
-        sq_on(1, 0, nc.vector)
         mx(0, 0)
         mx(0, 1)
-        xt(1, 0, rb[1])
+        xt(1, 1, xb[0])
+        sq_far(1, 0, mb[3])
         ars(0, 0)
         ars(0, 1)
-        out_words(1, 0, rb[1])
+        sq_turned(1, xb[0])
+        sq_nat(2, nc.vector)
         g_less(1)
         g_quant(1)
-        sq_on(1, 1, nc.vector)
+        sq_nat(3, nc.vector)
+        sq_nat(4, nc.vector)
         mx(0, 2)
         mx(0, 3)
-        xt(1, 1, rb[2])
+        xt(2, 0, mb[0])
         ars(0, 2)
         ars(0, 3)
-        out_words(1, 1, rb[2])
-        sq_on(2, 0, nc.vector)
-        sq_on(2, 1, nc.vector)
-        xt(2, 0, mb[0])
         xt(2, 1, xb[0])
-        out_words(2, 0, mb[0])
-        out_words(2, 1, xb[0])
-        sq_on(3, 0, nc.vector)
-        sq_on(3, 1, nc.vector)
+        words_back(2, mb[0])
+        sq_nat(5, nc.vector)
         quant(1)
-        sq_on(4, 0, nc.vector)
-        sq_on(4, 1, nc.vector)
-        sq_on(5, 0, nc.vector)
-        sq_on(5, 1, nc.vector)
-        for k in range(1, NCH + 1):
+        sq_turned(2, xb[0])
+        xt(3, 0, rb[2])
+        words_back(3, rb[2])
+        quant(2)
+        for m in range(4):
+            mx(1, m)
+        rtr(0)
+        xt(3, 1, xb[0])
+        rtr(1)
+        ars(1, 0)
+        xt(4, 0, mb[0])
+        rtr(2)
+        mul(0)
+        mul(1)
+        mul(2)
+        ars(1, 1)
+        ars(1, 2)
+        sq_turned(3, xb[0])
+        ars(1, 3)
+        xt(4, 1, xb[0])
+        words_back(4, mb[0])
+        sq_turned(4, xb[0])
+        sq_nat(6, nc.vector)
+        quant(3)
+        sq_nat(7, nc.gpsimd)
+        for k in range(2, NCH + 2):
             for m in range(4):
                 mx(k, m)
-            rtr(k - 1, 0)
             ars(k, 0)
-            xt(k + 2, 0, mb[0])
-            rtr(k - 1, 1)
-            rtr(k - 1, 2)
-            xt(k + 2, 1, xb[0])
-            ars(k, 1)
-            ars(k, 2)
-            out_words(k + 2, 0, mb[0])
-            ars(k, 3)
-            out_words(k + 2, 1, xb[0])
-            mul(k - 1, 0)
-            if k == 1:
-                quant(2)
-            rtr(k - 1, 3)
-            mul(k - 1, 1)
-            mul(k - 1, 2)
-            mul(k - 1, 3)
-            sq_on(k + 1 + NSQ, 0, nc.vector)
-            sq_tile(k + 1 + NSQ, 2, nc.vector)
-            sq_tile(k + 1 + NSQ, 3, nc.gpsimd)
+            rtr(4 * k - 5)
+            mul(4 * k - 5)
+            xt(k + 3, 0, mb[0])
+            words_back(k + 3, mb[0])
             quant(k + 2)
+            sq_nat(k + 6, nc.gpsimd)
+            xt(k + 3, 1, xb[0])
+            for j in range(4 * k - 4, 4 * k - 1):
+                rtr(j)
+            for m in range(1, 4):
+                ars(k, m)
+            sq_turned(k + 3, xb[0])
+            for j in range(4 * k - 4, 4 * k - 1):
+                mul(j)

@@ -23,7 +23,7 @@ GAMMA_BOUND = 2.0 ** -18
 BETA_BOUND = (1e-6 + PEDESTAL) ** 0.5
 RUN = 16
 
-NSQ = 5
+NSQ = 3
 NCD = 3
 NRT = 3
 NO = 4
@@ -56,8 +56,8 @@ def tile_gdn_t_kernel(tc, x, beta, gamma, out):
         rt = [keep.tile([P, 4, CHUNK], F32, name="rt%d" % i) for i in range(NRT)]
         ot = [keep.tile([P, 4, CH], F32, name="ot%d" % i) for i in range(NO)]
 
-        xb = [psum.tile([P, 512], F32, name="xb%d" % i) for i in range(1)]
-        mb = [psum.tile([P, 512], F32, name="mb%d" % i) for i in range(4)]
+        xb = [psum.tile([P, 512], F32, name="xb%d" % i) for i in range(2)]
+        mb = [psum.tile([P, 512], F32, name="mb%d" % i) for i in range(3)]
         rb = [psum.tile([P, 512], F32, name="rb%d" % i) for i in range(3)]
 
         xv = x.rearrange("(c p r) j -> c p r j", p=P, r=4)
@@ -156,14 +156,14 @@ def tile_gdn_t_kernel(tc, x, beta, gamma, out):
         def mx(c, m):
             if ok(c):
                 cols = slice(m * P, (m + 1) * P)
-                nc.tensor.matmul_mx(out=mb[m][:],
+                nc.tensor.matmul_mx(out=mb[(4 * c + m) % 3][:],
                                     lhsT=g_cd[:, cols].bitcast(FP8X4), lhsT_scale=g_sc[:, cols],
                                     rhs=cd[c % NCD][:].bitcast(FP8X4), rhs_scale=sc[c % NCD][:],
                                     start=True, stop=True)
 
         def ars(c, m):
             if ok(c):
-                nc.scalar.activation(out=rt[c % NRT][:, m, :], in_=mb[m][:],
+                nc.scalar.activation(out=rt[c % NRT][:, m, :], in_=mb[(4 * c + m) % 3][:],
                                      func=ACT.Abs_reciprocal_sqrt, bias=b_sb[:, m:m + 1], scale=1.0)
 
         def rtr(j):
@@ -204,80 +204,59 @@ def tile_gdn_t_kernel(tc, x, beta, gamma, out):
         sq_nat(0, nc.vector)
         g_max(1)
         bias_square()
-        turn(mb[1], half(gq, 0))
-        xt(0, 0, mb[0])
-        g_square(0, mb[1])
-        xt(0, 1, xb[0])
-        sq_turned(0, xb[0])
-        words_back(0, mb[0])
+        turn(mb[2], half(gq, 0))
+        xt(0, 0, xb[0])
+        g_square(0, mb[2])
+        xt(0, 1, xb[1])
+        sq_turned(0, xb[1])
+        words_back(0, xb[0])
         bias_less()
-        turn(mb[2], half(gq, 1))
-        xt_far(1, 0, mb[3])
-        g_square(1, mb[2])
+        turn(rb[1], half(gq, 1))
+        xt_far(1, 0, rb[2])
+        g_square(1, rb[1])
         g_less(0)
         g_quant(0)
         quant(0)
         mx(0, 0)
         mx(0, 1)
-        xt(1, 1, xb[0])
-        sq_far(1, 0, mb[3])
+        xt(1, 1, xb[1])
+        sq_far(1, 0, rb[2])
         ars(0, 0)
         ars(0, 1)
-        sq_turned(1, xb[0])
+        sq_turned(1, xb[1])
         sq_nat(2, nc.vector)
         g_less(1)
         g_quant(1)
-        sq_nat(3, nc.vector)
-        sq_nat(4, nc.vector)
         mx(0, 2)
         mx(0, 3)
-        xt(2, 0, mb[0])
+        xt(2, 0, xb[0])
+        xt(2, 1, xb[1])
         ars(0, 2)
         ars(0, 3)
-        xt(2, 1, xb[0])
-        words_back(2, mb[0])
-        sq_nat(5, nc.vector)
+        words_back(2, xb[0])
+        sq_nat(3, nc.vector)
         quant(1)
-        sq_turned(2, xb[0])
-        xt(3, 0, rb[2])
-        words_back(3, rb[2])
-        quant(2)
-        for m in range(4):
-            mx(1, m)
-        rtr(0)
-        xt(3, 1, xb[0])
-        rtr(1)
-        ars(1, 0)
-        xt(4, 0, mb[0])
-        rtr(2)
-        mul(0)
-        mul(1)
-        mul(2)
-        ars(1, 1)
-        ars(1, 2)
-        sq_turned(3, xb[0])
-        ars(1, 3)
-        xt(4, 1, xb[0])
-        words_back(4, mb[0])
-        sq_turned(4, xb[0])
-        sq_nat(6, nc.vector)
-        quant(3)
-        sq_nat(7, nc.gpsimd)
-        for k in range(2, NCH + 2):
-            for m in range(4):
-                mx(k, m)
+        sq_nat(4, nc.gpsimd)
+        for k in range(1, NCH + 1):
+            sq_turned(k + 1, xb[1])
+            mx(k, 0)
+            mx(k, 1)
+            xt(k + 2, 0, xb[0])
+            words_back(k + 2, xb[0])
+            quant(k + 1)
+            sq_nat(k + 1 + NSQ, nc.gpsimd)
+            rtr(4 * k - 4)
+            rtr(4 * k - 3)
             ars(k, 0)
-            rtr(4 * k - 5)
-            mul(4 * k - 5)
-            xt(k + 3, 0, mb[0])
-            words_back(k + 3, mb[0])
-            quant(k + 2)
-            sq_nat(k + 6, nc.gpsimd)
-            xt(k + 3, 1, xb[0])
-            for j in range(4 * k - 4, 4 * k - 1):
-                rtr(j)
-            for m in range(1, 4):
-                ars(k, m)
-            sq_turned(k + 3, xb[0])
-            for j in range(4 * k - 4, 4 * k - 1):
-                mul(j)
+            ars(k, 1)
+            mul(4 * k - 4)
+            mul(4 * k - 3)
+            mx(k, 2)
+            mx(k, 3)
+            ars(k, 2)
+            ars(k, 3)
+            rtr(4 * k - 2)
+            xt(k + 2, 1, xb[1])
+            rtr(4 * k - 1)
+            mul(4 * k - 2)
+            mul(4 * k - 1)

@@ -23,8 +23,8 @@ GAMMA_BOUND = 2.0 ** -18
 BETA_BOUND = (1e-6 + PEDESTAL) ** 0.5
 RUN = 16
 
-NSQ = 3
-NCD = 3
+NSQ = 5
+NCD = 4
 NRT = 3
 NO = 4
 
@@ -212,51 +212,82 @@ def tile_gdn_t_kernel(tc, x, beta, gamma, out):
         words_back(0, xb[0])
         bias_less()
         turn(rb[1], half(gq, 1))
-        xt_far(1, 0, rb[2])
+        xt(1, 1, rb[0])
         g_square(1, rb[1])
+        sq_turned(1, rb[0])
+        sq_nat(1, nc.vector)
         g_less(0)
+        xt(1, 0, xb[0])
+        xt(2, 1, rb[2])
         g_quant(0)
         quant(0)
+        words_back(1, xb[0])
         mx(0, 0)
         mx(0, 1)
-        xt(1, 1, xb[1])
-        sq_far(1, 0, rb[2])
         ars(0, 0)
         ars(0, 1)
-        sq_turned(1, xb[1])
-        sq_nat(2, nc.vector)
+        sq_turned(2, rb[2])
         g_less(1)
+        sq_nat(2, nc.vector)
         g_quant(1)
+        quant(1)
+        xt(2, 0, xb[0])
         mx(0, 2)
         mx(0, 3)
-        xt(2, 0, xb[0])
-        xt(2, 1, xb[1])
         ars(0, 2)
         ars(0, 3)
-        words_back(2, xb[0])
         sq_nat(3, nc.vector)
-        quant(1)
-        sq_nat(4, nc.gpsimd)
-        for k in range(1, NCH + 1):
-            sq_turned(k + 1, xb[1])
+        words_back(2, xb[0])
+        sq_nat(4, nc.vector)
+        sq_nat(5, nc.vector)
+        quant(2)
+        xt(3, 1, xb[1])
+        mx(1, 0)
+        mx(1, 1)
+        xt(3, 0, xb[0])
+        rtr(0)
+        rtr(1)
+        words_back(3, xb[0])
+        mul(0)
+        mul(1)
+        ars(1, 0)
+        ars(1, 1)
+        sq_turned(3, xb[1])
+        mx(1, 2)
+        mx(1, 3)
+        xt(4, 0, xb[0])
+        xt(4, 1, xb[1])
+        rtr(2)
+        rtr(3)
+        words_back(4, xb[0])
+        ars(1, 2)
+        ars(1, 3)
+        sq_nat(6, nc.vector)
+        quant(3)
+        sq_nat(7, nc.gpsimd)
+        sq_nat(8, nc.gpsimd)
+        mul(2)
+        mul(3)
+        for k in range(2, NCH + 1):
             mx(k, 0)
             mx(k, 1)
-            xt(k + 2, 0, xb[0])
-            words_back(k + 2, xb[0])
-            quant(k + 1)
-            sq_nat(k + 1 + NSQ, nc.gpsimd)
-            rtr(4 * k - 4)
-            rtr(4 * k - 3)
+            sq_turned(k + 2, xb[1])
             ars(k, 0)
             ars(k, 1)
+            xt(k + 3, 0, xb[0])
+            rtr(4 * k - 4)
+            rtr(4 * k - 3)
             mul(4 * k - 4)
             mul(4 * k - 3)
+            words_back(k + 3, xb[0])
+            quant(k + 2)
+            sq_nat(k + 7, nc.gpsimd)
             mx(k, 2)
             mx(k, 3)
             ars(k, 2)
             ars(k, 3)
+            xt(k + 3, 1, xb[1])
             rtr(4 * k - 2)
-            xt(k + 2, 1, xb[1])
             rtr(4 * k - 1)
             mul(4 * k - 2)
             mul(4 * k - 1)

@@ -153,29 +153,42 @@ def tile_gdn_t_kernel(tc, x, beta, gamma, out):
             if ok(c):
                 nc.vector.quantize_mx(out=cd[c % NCD][:].bitcast(FP8X4), scales=sc[c % NCD][:], in_=sq[c % NSQ][:])
 
+        late = [mb[0], mb[1], mb[2], xb[1]]
+
+        def mbank(c, m):
+            if c >= NCH - 2:
+                return late[(4 * (c - NCH + 2) + m) % 4]
+            return mb[(4 * c + m) % 3]
+
         def mx(c, m):
             if ok(c):
                 cols = slice(m * P, (m + 1) * P)
-                nc.tensor.matmul_mx(out=mb[(4 * c + m) % 3][:],
+                nc.tensor.matmul_mx(out=mbank(c, m)[:],
                                     lhsT=g_cd[:, cols].bitcast(FP8X4), lhsT_scale=g_sc[:, cols],
                                     rhs=cd[c % NCD][:].bitcast(FP8X4), rhs_scale=sc[c % NCD][:],
                                     start=True, stop=True)
 
         def ars(c, m):
             if ok(c):
-                nc.scalar.activation(out=rt[c % NRT][:, m, :], in_=mb[(4 * c + m) % 3][:],
+                nc.scalar.activation(out=rt[c % NRT][:, m, :], in_=mbank(c, m)[:],
                                      func=ACT.Abs_reciprocal_sqrt, bias=b_sb[:, m:m + 1], scale=1.0)
+
+        def rbank(j):
+            late = j - 4 * (NCH - 3)
+            if late >= 0:
+                return (rb + [xb[0]])[(late + 2) % 4]
+            return rb[j % 3]
 
         def rtr(j):
             c, r = divmod(j, 4)
             if ok(c):
                 for m in range(4):
-                    nc.tensor.transpose(rb[j % 3][:, m * P:(m + 1) * P], rt[c % NRT][:, m, r * P:(r + 1) * P], ident[:])
+                    nc.tensor.transpose(rbank(j)[:, m * P:(m + 1) * P], rt[c % NRT][:, m, r * P:(r + 1) * P], ident[:])
 
         def mul(j):
             c, r = divmod(j, 4)
             if ok(c):
-                nc.vector.tensor_tensor(out=ot[c % NO][:, r, :], in0=rb[j % 3][:], in1=xs[c][:, r, :],
+                nc.vector.tensor_tensor(out=ot[c % NO][:, r, :], in0=rbank(j)[:], in1=xs[c][:, r, :],
                                         op=ALU.mult)
                 if c == NCH - 1:
                     store(c, r, r + 1)
@@ -200,22 +213,22 @@ def tile_gdn_t_kernel(tc, x, beta, gamma, out):
 
         bias_turn()
         g_max(0)
-        bias_max()
         sq_nat(0, nc.vector)
         g_max(1)
-        bias_square()
+        bias_max()
         turn(mb[2], half(gq, 0))
         xt(0, 0, xb[0])
         g_square(0, mb[2])
         xt(0, 1, xb[1])
         sq_turned(0, xb[1])
         words_back(0, xb[0])
-        bias_less()
+        bias_square()
         turn(rb[1], half(gq, 1))
         xt(1, 1, rb[0])
         g_square(1, rb[1])
         sq_turned(1, rb[0])
         sq_nat(1, nc.vector)
+        bias_less()
         g_less(0)
         xt(1, 0, xb[0])
         xt(2, 1, rb[2])
@@ -271,23 +284,23 @@ def tile_gdn_t_kernel(tc, x, beta, gamma, out):
         for k in range(2, NCH + 1):
             mx(k, 0)
             mx(k, 1)
-            sq_turned(k + 2, xb[1])
-            ars(k, 0)
-            ars(k, 1)
             xt(k + 3, 0, xb[0])
             rtr(4 * k - 4)
             rtr(4 * k - 3)
+            mx(k, 2)
+            sq_turned(k + 2, xb[1])
+            ars(k, 0)
+            ars(k, 1)
+            ars(k, 2)
+            words_back(k + 3, xb[0])
             mul(4 * k - 4)
             mul(4 * k - 3)
-            words_back(k + 3, xb[0])
             quant(k + 2)
             sq_nat(k + 7, nc.gpsimd)
-            mx(k, 2)
             mx(k, 3)
-            ars(k, 2)
-            ars(k, 3)
             xt(k + 3, 1, xb[1])
             rtr(4 * k - 2)
             rtr(4 * k - 1)
+            ars(k, 3)
             mul(4 * k - 2)
             mul(4 * k - 1)

from contextlib import ExitStack

import concourse.masks as masks
import concourse.mybir as mybir

F32 = mybir.dt.float32
BF16 = mybir.dt.bfloat16
U32 = mybir.dt.uint32
U8 = mybir.dt.uint8
FP8X4 = mybir.dt.float8_e4m3fn_x4
ACT = mybir.ActivationFunctionType
ALU = mybir.AluOpType

P = 128
N_ROWS = 10240
CH = 512
CHUNK = 512
NCH = N_ROWS // CHUNK
FLOPS = 2 * N_ROWS * CH * CH

PEDESTAL = 2.0 ** -36
GAMMA_BOUND = 2.0 ** -18
BETA_BOUND = (1e-6 + PEDESTAL) ** 0.5
RUN = 16

NSQ = 5
NCD = 4
NRT = 3
NO = 4


def tile_gdn_t_kernel(tc, x, beta, gamma, out):
    nc = tc.nc
    with ExitStack() as ctx:
        keep = ctx.enter_context(tc.tile_pool(name="keep", bufs=1))
        psum = ctx.enter_context(tc.psum_pool(name="psum", bufs=1))
        ctx.enter_context(tc.manual_schedule())

        ident = keep.tile([P, P], F32, name="ident")
        warm = keep.tile([P, 1], F32, name="warm")
        warm2 = keep.tile([P, 1], F32, name="warm2")
        gam = keep.tile([P, 4, CH], BF16, name="gam")
        bet = keep.tile([4, P], BF16, name="bet")
        bz = keep.tile([P, P], F32, name="bz")
        b1 = keep.tile([P, 4], F32, name="b1")
        b2 = keep.tile([P, 4], F32, name="b2")
        b_sb = keep.tile([P, 4], F32, name="b_sb")
        g2 = [keep.tile([P, 1024], F32, name="g2%d" % i) for i in range(2)]
        gq = keep.tile([P, 2048], BF16, name="gq", align_bytes=64)
        g_cd = keep.tile([P, CH], U32, name="g_cd", align_bytes=64)
        g_sc = keep.tile([P, CH], U8, name="g_sc", align_bytes=64)
        xs = [keep.tile([P, 4, CH], BF16, name="x%d" % c) for c in range(NCH)]
        sq = [keep.tile([P, 2048], BF16, name="sq%d" % i, align_bytes=64) for i in range(NSQ)]
        cd = [keep.tile([P, CHUNK], U32, name="cd%d" % i, align_bytes=64) for i in range(NCD)]
        sc = [keep.tile([P, CHUNK], U8, name="sc%d" % i, align_bytes=64) for i in range(NCD)]
        rt = [keep.tile([P, 4, CHUNK], F32, name="rt%d" % i) for i in range(NRT)]
        ot = [keep.tile([P, 4, CH], F32, name="ot%d" % i) for i in range(NO)]

        xb = [psum.tile([P, 512], F32, name="xb%d" % i) for i in range(2)]
        mb = [psum.tile([P, 512], F32, name="mb%d" % i) for i in range(3)]
        rb = [psum.tile([P, 512], F32, name="rb%d" % i) for i in range(3)]

        xv = x.rearrange("(c p r) j -> c p r j", p=P, r=4)
        ov = out.rearrange("(c p r) i -> c p r i", p=P, r=4)
        gv = gamma.rearrange("(m p) j -> p m j", p=P)

        nc.scalar.dma_start(out=bet[:], in_=beta.rearrange("(m p) -> m p", p=P))
        nc.sync.dma_start(out=gam[:, 0:2, :], in_=gv[:, 0:2, :])
        nc.sync.dma_start(out=xs[0][:, 0:2, :], in_=xv[0, :, 0:2, :])
        nc.sync.dma_start(out=gam[:, 2:4, :], in_=gv[:, 2:4, :])
        nc.sync.dma_start(out=xs[0][:, 2:4, :], in_=xv[0, :, 2:4, :])
        for c in range(1, NCH):
            nc.sync.dma_start(out=xs[c][:], in_=xv[c, :, :, :])

        masks.make_identity(nc, ident[:])
        nc.vector.memset(warm[:], 1.0)
        nc.scalar.activation(out=warm2[:], in_=warm[:], func=ACT.Abs_reciprocal_sqrt)
        nc.vector.memset(bz[:], 0.0)

        def bias_turn():
            nc.vector.tensor_copy(out=bz[0:4, :], in_=bet[:])
            nc.tensor.transpose(rb[0][:, 0:P], bz[:], ident[:])

        def bias_max():
            nc.vector.tensor_scalar_max(out=b1[:], in0=rb[0][:, 0:4], scalar1=BETA_BOUND)

        def bias_square():
            nc.vector.tensor_tensor(out=b2[:], in0=b1[:], in1=b1[:], op=ALU.mult)

        def bias_less():
            nc.vector.tensor_scalar_add(out=b_sb[:], in0=b2[:], scalar1=-PEDESTAL)

        def flat(pair):
            return pair.rearrange("p r j -> p (r j)")

        def half(t, h):
            return t[:, h * 1024:(h + 1) * 1024]

        def turn_near(bank, rows):
            for b in range(4):
                nc.tensor.transpose(bank[:, b * P:(b + 1) * P], rows.bitcast(F32)[:, b * P:(b + 1) * P], ident[:])

        def turn(bank, rows):
            words = rows.bitcast(F32)
            for u in range(2):
                for t in range(2):
                    nc.tensor.transpose(bank[:, (2 * u + t) * P:(2 * u + t + 1) * P],
                                        words[:, 256 * t + u:256 * (t + 1):2], ident[:])

        def bank_words(bank):
            return bank[:].rearrange("p (u n) -> p n u", u=2)

        def grouped_words(dst):
            return dst.bitcast(F32).rearrange("p (n u) -> p n u", u=2)

        def grouped(dst):
            return dst.rearrange("p (n u e) -> p n u e", u=2, e=2)

        def bank_pairs(bank):
            return bank[:].bitcast(BF16).rearrange("p (u n e) -> p n u e", u=2, e=2)

        def ok(c):
            return 0 <= c < NCH

        def sq_nat(c, eng):
            if ok(c):
                src = flat(xs[c][:, 0:2, :]).rearrange("p (w u e) -> p u w e", u=2, e=2)
                dst = half(sq[c % NSQ], 0).rearrange("p (u w e) -> p u w e", u=2, e=2)
                eng.tensor_tensor(out=dst, in0=src, in1=src, op=ALU.mult)

        def xt(c, h, bank):
            if ok(c):
                if h == 0:
                    turn_near(bank, half(sq[c % NSQ], 0))
                else:
                    turn(bank, flat(xs[c][:, 2:4, :]))

        def xt_far(c, h, bank):
            turn(bank, flat(xs[c][:, 2 * h:2 * h + 2, :]))

        def sq_far(c, h, bank):
            nc.scalar.activation(out=grouped(half(sq[c % NSQ], h)), in_=bank_pairs(bank), func=ACT.Square)

        def words_back(c, bank):
            if ok(c):
                nc.vector.tensor_copy(out=grouped_words(half(sq[c % NSQ], 0)), in_=bank_words(bank))

        def sq_turned(c, bank):
            if ok(c):
                nc.scalar.activation(out=grouped(half(sq[c % NSQ], 1)), in_=bank_pairs(bank), func=ACT.Square)

        def quant(c):
            if ok(c):
                nc.vector.quantize_mx(out=cd[c % NCD][:].bitcast(FP8X4), scales=sc[c % NCD][:], in_=sq[c % NSQ][:])

        late = [mb[0], mb[1], mb[2], xb[1]]

        def mbank(c, m):
            if c >= NCH - 2:
                return late[(4 * (c - NCH + 2) + m) % 4]
            return mb[(4 * c + m) % 3]

        def mx(c, m):
            if ok(c):
                cols = slice(m * P, (m + 1) * P)
                nc.tensor.matmul_mx(out=mbank(c, m)[:],
                                    lhsT=g_cd[:, cols].bitcast(FP8X4), lhsT_scale=g_sc[:, cols],
                                    rhs=cd[c % NCD][:].bitcast(FP8X4), rhs_scale=sc[c % NCD][:],
                                    start=True, stop=True)

        def ars(c, m):
            if ok(c):
                nc.scalar.activation(out=rt[c % NRT][:, m, :], in_=mbank(c, m)[:],
                                     func=ACT.Abs_reciprocal_sqrt, bias=b_sb[:, m:m + 1], scale=1.0)

        def rbank(j):
            late = j - 4 * (NCH - 3)
            if late >= 0:
                return (rb + [xb[0]])[(late + 2) % 4]
            return rb[j % 3]

        def rtr(j):
            c, r = divmod(j, 4)
            if ok(c):
                for m in range(4):
                    nc.tensor.transpose(rbank(j)[:, m * P:(m + 1) * P], rt[c % NRT][:, m, r * P:(r + 1) * P], ident[:])

        def mul(j):
            c, r = divmod(j, 4)
            if ok(c):
                nc.vector.tensor_tensor(out=ot[c % NO][:, r, :], in0=rbank(j)[:], in1=xs[c][:, r, :],
                                        op=ALU.mult)
                if c == NCH - 1:
                    store(c, r, r + 1)
                elif r % 2 == 1:
                    store(c, r - 1, r + 1)

        def store(c, r0, r1):
            nc.sync.dma_start(out=ov[c, :, r0:r1, :], in_=ot[c % NO][:, r0:r1, :])

        def g_max(h):
            nc.vector.tensor_scalar_max(out=half(gq, h), in0=flat(gam[:, 2 * h:2 * h + 2, :]), scalar1=GAMMA_BOUND)

        def g_square(h, bank):
            nc.scalar.activation(out=grouped(g2[h][:]), in_=bank_pairs(bank), func=ACT.Square)

        def g_less(h):
            nc.vector.tensor_scalar_add(out=half(gq, h), in0=g2[h][:], scalar1=-PEDESTAL)

        def g_quant(h):
            wcols = slice(h * 256, (h + 1) * 256)
            nc.vector.quantize_mx(out=g_cd[:, wcols].bitcast(FP8X4), scales=g_sc[:, wcols], in_=half(gq, h))

        bias_turn()
        g_max(0)
        sq_nat(0, nc.vector)
        g_max(1)
        bias_max()
        turn(mb[2], half(gq, 0))
        xt(0, 0, xb[0])
        g_square(0, mb[2])
        xt(0, 1, xb[1])
        sq_turned(0, xb[1])
        words_back(0, xb[0])
        bias_square()
        turn(rb[1], half(gq, 1))
        xt(1, 1, rb[0])
        g_square(1, rb[1])
        sq_turned(1, rb[0])
        sq_nat(1, nc.vector)
        bias_less()
        g_less(0)
        xt(1, 0, xb[0])
        xt(2, 1, rb[2])
        g_quant(0)
        quant(0)
        words_back(1, xb[0])
        mx(0, 0)
        mx(0, 1)
        ars(0, 0)
        ars(0, 1)
        sq_turned(2, rb[2])
        g_less(1)
        sq_nat(2, nc.vector)
        g_quant(1)
        quant(1)
        xt(2, 0, xb[0])
        mx(0, 2)
        mx(0, 3)
        ars(0, 2)
        ars(0, 3)
        sq_nat(3, nc.vector)
        words_back(2, xb[0])
        sq_nat(4, nc.vector)
        sq_nat(5, nc.vector)
        quant(2)
        xt(3, 1, xb[1])
        mx(1, 0)
        mx(1, 1)
        xt(3, 0, xb[0])
        rtr(0)
        rtr(1)
        words_back(3, xb[0])
        mul(0)
        mul(1)
        ars(1, 0)
        ars(1, 1)
        sq_turned(3, xb[1])
        mx(1, 2)
        mx(1, 3)
        xt(4, 0, xb[0])
        xt(4, 1, xb[1])
        rtr(2)
        rtr(3)
        words_back(4, xb[0])
        ars(1, 2)
        ars(1, 3)
        sq_nat(6, nc.vector)
        quant(3)
        sq_nat(7, nc.gpsimd)
        sq_nat(8, nc.gpsimd)
        mul(2)
        mul(3)
        for k in range(2, NCH + 1):
            mx(k, 0)
            mx(k, 1)
            xt(k + 3, 0, xb[0])
            rtr(4 * k - 4)
            rtr(4 * k - 3)
            mx(k, 2)
            sq_turned(k + 2, xb[1])
            ars(k, 0)
            ars(k, 1)
            ars(k, 2)
            words_back(k + 3, xb[0])
            mul(4 * k - 4)
            mul(4 * k - 3)
            quant(k + 2)
            sq_nat(k + 7, nc.gpsimd)
            mx(k, 3)
            xt(k + 3, 1, xb[1])
            rtr(4 * k - 2)
            rtr(4 * k - 1)
            ars(k, 3)
            mul(4 * k - 2)
            mul(4 * k - 1)
